import numpy as np
import ml_dtypes


def mxq(x, axis, fmt="e4m3"):
    dtype, down = {"e4m3": (ml_dtypes.float8_e4m3fn, 7), "e5m2": (ml_dtypes.float8_e5m2, 14)}[fmt]
    v = np.moveaxis(np.asarray(x, np.float32).astype(ml_dtypes.bfloat16).astype(np.float64), axis, -1)
    blocks = v.reshape(v.shape[:-1] + (-1, 32))
    amax = np.abs(blocks).max(-1, keepdims=True)
    byte = np.maximum(np.where(amax > 0, np.frexp(amax)[1] - 1 + 127, 0) - down, 1)
    scale = np.exp2(byte - 127.0)
    codes = (blocks / scale).astype(np.float32).astype(dtype).astype(np.float64)
    return np.moveaxis((codes * scale).reshape(v.shape), -1, axis)


WIDE = False


def mx_kscale(k):
    if not WIDE:
        return np.ones(k)
    levels = np.array([10, -10, 5, -5, 0])
    a = np.random.permutation(np.resize(levels, k // 512 * 4)).reshape(k // 512, 4)
    idx = np.arange(k)
    return np.exp2(a[idx // 512, idx % 128 // 32])


BF16 = ml_dtypes.bfloat16


def bf(x):
    return np.asarray(x, np.float32).astype(BF16)


def f64(x):
    return np.asarray(x).astype(np.float64)


N, C, F, G = 4096, 3, 128, 512
F2 = F + F
F3 = F2 + F


def silu(v):
    return v / (1.0 + np.exp(-v))


def setup_inputs():
    s = mx_kscale(G)
    return {"h": bf(silu(1.4 * np.random.standard_normal((N, 1, G))) * s),
            "mu_W": bf(np.random.standard_normal((N, C, F))),
            "mu_VW": bf(np.sqrt(C) * np.random.standard_normal((N, 1, F))),
            "q": bf(np.random.standard_normal((N, 1, F))),
            "mu": bf(np.random.standard_normal((N, C, F))),
            "W2": bf(np.random.standard_normal((F3, G)) / np.sqrt(G) / s),
            "b2": bf(0.2 * np.random.standard_normal(F3))}


def reference(h, mu_W, mu_VW, q, mu, W2, b2):
    x = (mxq(f64(h), 2, "e4m3") @ mxq(f64(W2), 1, "e4m3").T) + f64(b2)
    dq_intra = x[..., :F]
    dmu_intra = x[..., F:F2] * f64(mu_W)
    dqmu_intra = x[..., F2:] * f64(mu_VW)
    q_out = f64(q) + dq_intra + dqmu_intra
    mu_out = f64(mu) + dmu_intra
    return q_out, mu_out

@@ -1,0 +1,197 @@
+from contextlib import ExitStack
+
+import concourse.mybir as mybir
+from concourse.masks import make_identity
+
+FLOPS = 2 * 4096 * 512 * 384
+
+F32 = mybir.dt.float32
+BF16 = mybir.dt.bfloat16
+U32 = mybir.dt.uint32
+U8 = mybir.dt.uint8
+FP8X4 = mybir.dt.float8_e4m3fn_x4
+MULT = mybir.AluOpType.mult
+ADD = mybir.AluOpType.add
+IDENTITY = mybir.ActivationFunctionType.Identity
+
+P = 128
+ATOMS = 4096
+G = 512
+F = 128
+C = 3
+TPP = ATOMS // P
+T = 4
+NCH = TPP // T
+BLOCK_ORDER = (1, 2, 0)
+
+
+def tile_painnmixing_pb_t_kernel(tc, h, mu_W, mu_VW, q, mu, W2, b2, out_0, out_1):
+    nc = tc.nc
+    h_v = h.rearrange("(p t) o k -> p (t o k)", t=TPP)
+    muw_v = mu_W.rearrange("(p t) c f -> p (t c f)", t=TPP)
+    muvw_v = mu_VW.rearrange("(p t) o f -> p (t o f)", t=TPP)
+    q_v = q.rearrange("(p t) o f -> p (t o f)", t=TPP)
+    mu_v = mu.rearrange("(p t) c f -> p (t c f)", t=TPP)
+    o0_v = out_0.rearrange("(p t) o f -> p (t o f)", t=TPP)
+    o1_v = out_1.rearrange("(p t) c f -> p (t c f)", t=TPP)
+
+    with ExitStack() as ctx:
+        consts = ctx.enter_context(tc.tile_pool(name="consts", bufs=1))
+        res = ctx.enter_context(tc.tile_pool(name="res", bufs=1))
+        work = ctx.enter_context(tc.tile_pool(name="work", bufs=2))
+        ps_a = ctx.enter_context(tc.psum_pool(name="ps_a", bufs=2))
+        ps_b = ctx.enter_context(tc.psum_pool(name="ps_b", bufs=3))
+        ps_c = ctx.enter_context(tc.psum_pool(name="ps_c", bufs=3))
+
+        bz = consts.tile([P, P], BF16, name="bz")
+        nc.vector.memset(bz[:], 0.0)
+        nc.scalar.dma_start(out=bz[0:3, :], in_=b2.rearrange("(j f) -> j f", j=3))
+        w_sb = consts.tile([P, 3 * G], BF16, name="w_sb")
+        nc.sync.dma_start(
+            out=w_sb[:].rearrange("p (j k) -> p j k", j=3),
+            in_=W2.rearrange("(j p) k -> p j k", p=P),
+        )
+        h_sb, muw_sb, muvw_sb, q_sb, mu_sb = [], [], [], [], []
+        for c in range(NCH):
+            t0 = c * T
+            ht = res.tile([P, T * G], BF16, name="h%d" % c)
+            nc.sync.dma_start(out=ht[:], in_=h_v[:, t0 * G:(t0 + T) * G])
+            h_sb.append(ht)
+            wt = res.tile([P, T * C * F], BF16, name="muw%d" % c)
+            nc.sync.dma_start(out=wt[:], in_=muw_v[:, t0 * C * F:(t0 + T) * C * F])
+            muw_sb.append(wt)
+            vt = res.tile([P, T * F], BF16, name="muvw%d" % c)
+            nc.sync.dma_start(out=vt[:], in_=muvw_v[:, t0 * F:(t0 + T) * F])
+            muvw_sb.append(vt)
+            qt = res.tile([P, T * F], BF16, name="q%d" % c)
+            nc.sync.dma_start(out=qt[:], in_=q_v[:, t0 * F:(t0 + T) * F])
+            q_sb.append(qt)
+            mt = res.tile([P, T * C * F], BF16, name="mu%d" % c)
+            nc.sync.dma_start(out=mt[:], in_=mu_v[:, t0 * C * F:(t0 + T) * C * F])
+            mu_sb.append(mt)
+
+        ident = consts.tile([P, P], F32, name="ident")
+        make_identity(nc, ident[:])
+
+        bzf = consts.tile([P, P], F32, name="bzf")
+        nc.vector.tensor_copy(out=bzf[:], in_=bz[:])
+        pb = ps_a.tile([P, 2, 256], F32, name="pb", tag="a")
+        nc.tensor.transpose(pb[:, 0, 0:P], bzf[:], ident[:])
+        bias = consts.tile([P, 4], F32, name="bias")
+        nc.vector.tensor_copy(out=bias[:, 0:3], in_=pb[:, 0, 0:3])
+
+        w32 = w_sb[:].bitcast(F32)
+        wg = consts.tile([P, 3 * G], BF16, name="wg", align_bytes=64)
+        wg32 = wg[:].bitcast(F32).rearrange("p (f u) -> p f u", u=2)
+        wc = consts.tile([P, 3 * F], U32, name="wc", align_bytes=64)
+        ws = consts.tile([P, 3 * F], U8, name="ws", align_bytes=64)
+        for f0, nj in ((0, 2), (2, 1)):
+            pw = ps_a.tile([P, 2, 256], F32, name="pw", tag="a")
+            for jl in range(nj):
+                for u in range(2):
+                    col = (f0 + jl) * 256 + u * P
+                    nc.tensor.transpose(pw[:, u, jl * P:(jl + 1) * P], w32[:, col:col + P], ident[:])
+            nc.vector.tensor_copy(
+                out=wg32[:, f0 * P:(f0 + nj) * P, :],
+                in_=pw[:, :, 0:nj * P].rearrange("p u a -> p a u"),
+            )
+        for f0, nj in ((0, 2), (2, 1)):
+            nc.vector.quantize_mx(
+                out=wc[:, f0 * P:(f0 + nj) * P].bitcast(FP8X4),
+                scales=ws[:, f0 * P:(f0 + nj) * P],
+                in_=wg[:, f0 * G:(f0 + nj) * G],
+            )
+
+        g_t, hc_t, hs_t, xb_t, c_t, mo_t, qo_t = {}, {}, {}, {}, {}, {}, {}
+
+        def fwd(c):
+            h32 = h_sb[c][:].bitcast(F32)
+            g = work.tile([P, T * G], BF16, name="g", tag="g", align_bytes=64)
+            g32 = g[:].bitcast(F32).rearrange("p (a u) -> p a u", u=2)
+            for hb in range(T // 2):
+                pa = ps_a.tile([P, 2, 256], F32, name="pa", tag="a")
+                for tl in range(2):
+                    for u in range(2):
+                        col = (hb * 2 + tl) * 256 + u * P
+                        nc.tensor.transpose(pa[:, u, tl * P:(tl + 1) * P], h32[:, col:col + P], ident[:])
+                nc.scalar.copy(
+                    out=g32[:, hb * 256:(hb + 1) * 256, :],
+                    in_=pa[:].rearrange("p u a -> p a u"),
+                )
+            g_t[c] = g
+
+        def quant(c):
+            hc = work.tile([P, T * P], U32, name="hc", tag="hc", align_bytes=64)
+            hs = work.tile([P, T * P], U8, name="hs", tag="hs", align_bytes=64)
+            nc.vector.quantize_mx(out=hc[:].bitcast(FP8X4), scales=hs[:], in_=g_t[c][:])
+            hc_t[c] = hc
+            hs_t[c] = hs
+
+        def mx(c):
+            xb = work.tile([P, 3, T * P], F32, name="xb", tag="xb")
+            for j in BLOCK_ORDER:
+                pbk = ps_b.tile([P, T * P], F32, name="pbk", tag="b")
+                nc.tensor.matmul_mx(
+                    out=pbk[:],
+                    lhsT=wc[:, j * P:(j + 1) * P].bitcast(FP8X4),
+                    lhsT_scale=ws[:, j * P:(j + 1) * P],
+                    rhs=hc_t[c][:].bitcast(FP8X4),
+                    rhs_scale=hs_t[c][:],
+                    start=True,
+                    stop=True,
+                )
+                nc.scalar.activation(out=xb[:, j, :], in_=pbk[:], func=IDENTITY, bias=bias[:, j:j + 1], scale=1.0)
+            xb_t[c] = xb
+
+        def back(c):
+            for j in BLOCK_ORDER:
+                pc = ps_c.tile([P, T, P], F32, name="pc", tag="c")
+                for t in range(T):
+                    nc.tensor.transpose(pc[:, t, :], xb_t[c][:, j, t * P:(t + 1) * P], ident[:])
+                c_t[(c, j)] = pc
+
+        def ew1(c):
+            mo = res.tile([P, T * C * F], F32, name="mo%d" % c)
+            qo = res.tile([P, T * F], F32, name="qo%d" % c)
+            v = work.tile([P, T * F], F32, name="v", tag="v")
+            nc.vector.tensor_tensor(
+                out=mo[:].rearrange("p (t c f) -> p t c f", t=T, c=C),
+                in0=c_t[(c, 1)][:].unsqueeze(2).to_broadcast([P, T, C, F]),
+                in1=muw_sb[c][:].rearrange("p (t c f) -> p t c f", t=T, c=C),
+                op=MULT,
+            )
+            nc.vector.tensor_tensor(
+                out=qo[:], in0=c_t[(c, 2)][:].rearrange("p t f -> p (t f)"), in1=muvw_sb[c][:], op=MULT
+            )
+            nc.vector.tensor_tensor(
+                out=v[:], in0=c_t[(c, 0)][:].rearrange("p t f -> p (t f)"), in1=q_sb[c][:], op=ADD
+            )
+            mo_t[c] = mo
+            qo_t[c] = (qo, v)
+
+        def ew2(c):
+            t0 = c * T
+            mo = mo_t[c]
+            qo, v = qo_t[c]
+            nc.vector.tensor_tensor(out=mo[:], in0=mo[:], in1=mu_sb[c][:], op=ADD)
+            nc.sync.dma_start(out=o1_v[:, t0 * C * F:(t0 + T) * C * F], in_=mo[:])
+            nc.vector.tensor_tensor(out=qo[:], in0=qo[:], in1=v[:], op=ADD)
+            nc.sync.dma_start(out=o0_v[:, t0 * F:(t0 + T) * F], in_=qo[:])
+
+        fwd(0)
+        quant(0)
+        fwd(1)
+        mx(0)
+        quant(1)
+        back(0)
+        for c in range(NCH):
+            if c + 2 < NCH:
+                fwd(c + 2)
+            if c + 1 < NCH:
+                mx(c + 1)
+            ew1(c)
+            if c + 2 < NCH:
+                quant(c + 2)
+            if c + 1 < NCH:
+                back(c + 1)
+            ew2(c)

@@ -20,9 +20,24 @@ G = 512
 F = 128
 C = 3
 TPP = ATOMS // P
-T = 4
-NCH = TPP // T
-BLOCK_ORDER = (1, 2, 0)
+CHUNKS = ((0, 2), (2, 2), (4, 4), (8, 4), (12, 4), (16, 4), (20, 4), (24, 4), (28, 2), (30, 2))
+NCH = len(CHUNKS)
+TMAX = 4
+
+H_PIECES = ((0, 2), (2, 4), (4, 8), (8, 12), (12, 20), (20, 28), (28, 32))
+VEC_PIECES = ((0, 2), (2, 4), (4, 8), (8, 12), (12, 20), (20, 28), (28, 32))
+SCA_PIECES = ((0, 4), (4, 12), (12, 32))
+MO_PIECES = ((0, 8), (8, 16), (16, 24), (24, 28), (28, 30), (30, 32))
+QO_PIECES = ((0, 16), (16, 28), (28, 32))
+LOAD_ORDER = (
+    ("h", 0), ("muw", 0), ("h", 1), ("q", 0), ("muvw", 0), ("mu", 0),
+    ("h", 2), ("muw", 1), ("mu", 1),
+    ("h", 3), ("muw", 2), ("q", 1), ("muvw", 1), ("mu", 2),
+    ("h", 4), ("muw", 3), ("mu", 3),
+    ("muw", 4), ("q", 2), ("muvw", 2), ("mu", 4),
+    ("h", 5), ("muw", 5), ("mu", 5),
+    ("h", 6), ("muw", 6), ("mu", 6),
+)
 
 
 def tile_painnmixing_pb_t_kernel(tc, h, mu_W, mu_VW, q, mu, W2, b2, out_0, out_1):
@@ -36,12 +51,34 @@ def tile_painnmixing_pb_t_kernel(tc, h, mu_W, mu_VW, q, mu, W2, b2, out_0, out_1
     o1_v = out_1.rearrange("(p t) c f -> p (t c f)", t=TPP)
 
     with ExitStack() as ctx:
+        ctx.enter_context(tc.manual_schedule())
         consts = ctx.enter_context(tc.tile_pool(name="consts", bufs=1))
         res = ctx.enter_context(tc.tile_pool(name="res", bufs=1))
         work = ctx.enter_context(tc.tile_pool(name="work", bufs=2))
         ps_a = ctx.enter_context(tc.psum_pool(name="ps_a", bufs=2))
         ps_b = ctx.enter_context(tc.psum_pool(name="ps_b", bufs=3))
-        ps_c = ctx.enter_context(tc.psum_pool(name="ps_c", bufs=3))
+        ps_c = ctx.enter_context(tc.psum_pool(name="ps_c", bufs=1))
+
+        def make_pieces(pieces, width, dtype, label):
+            return [
+                (ts, te, res.tile([P, (te - ts) * width], dtype, name="%s%d" % (label, ts)))
+                for ts, te in pieces
+            ]
+
+        def chunk_view(tiles, c, width):
+            t0, nt = CHUNKS[c]
+            for ts, te, tl in tiles:
+                if ts <= t0 and t0 + nt <= te:
+                    return tl[:, (t0 - ts) * width:(t0 - ts + nt) * width]
+            raise ValueError("chunk not inside a piece")
+
+        h_p = make_pieces(H_PIECES, G, BF16, "h")
+        muw_p = make_pieces(VEC_PIECES, C * F, BF16, "muw")
+        mu_p = make_pieces(VEC_PIECES, C * F, BF16, "mu")
+        muvw_p = make_pieces(SCA_PIECES, F, BF16, "muvw")
+        q_p = make_pieces(SCA_PIECES, F, BF16, "q")
+        mo_p = make_pieces(MO_PIECES, C * F, F32, "mo")
+        qo_p = make_pieces(QO_PIECES, F, F32, "qo")
 
         bz = consts.tile([P, P], BF16, name="bz")
         nc.vector.memset(bz[:], 0.0)
@@ -51,35 +88,28 @@ def tile_painnmixing_pb_t_kernel(tc, h, mu_W, mu_VW, q, mu, W2, b2, out_0, out_1
             out=w_sb[:].rearrange("p (j k) -> p j k", j=3),
             in_=W2.rearrange("(j p) k -> p j k", p=P),
         )
-        h_sb, muw_sb, muvw_sb, q_sb, mu_sb = [], [], [], [], []
-        for c in range(NCH):
-            t0 = c * T
-            ht = res.tile([P, T * G], BF16, name="h%d" % c)
-            nc.sync.dma_start(out=ht[:], in_=h_v[:, t0 * G:(t0 + T) * G])
-            h_sb.append(ht)
-            wt = res.tile([P, T * C * F], BF16, name="muw%d" % c)
-            nc.sync.dma_start(out=wt[:], in_=muw_v[:, t0 * C * F:(t0 + T) * C * F])
-            muw_sb.append(wt)
-            vt = res.tile([P, T * F], BF16, name="muvw%d" % c)
-            nc.sync.dma_start(out=vt[:], in_=muvw_v[:, t0 * F:(t0 + T) * F])
-            muvw_sb.append(vt)
-            qt = res.tile([P, T * F], BF16, name="q%d" % c)
-            nc.sync.dma_start(out=qt[:], in_=q_v[:, t0 * F:(t0 + T) * F])
-            q_sb.append(qt)
-            mt = res.tile([P, T * C * F], BF16, name="mu%d" % c)
-            nc.sync.dma_start(out=mt[:], in_=mu_v[:, t0 * C * F:(t0 + T) * C * F])
-            mu_sb.append(mt)
+        sources = {
+            "h": (h_p, h_v, G),
+            "muw": (muw_p, muw_v, C * F),
+            "mu": (mu_p, mu_v, C * F),
+            "muvw": (muvw_p, muvw_v, F),
+            "q": (q_p, q_v, F),
+        }
+        for key, i in LOAD_ORDER:
+            tiles, view, width = sources[key]
+            ts, te, tl = tiles[i]
+            nc.sync.dma_start(out=tl[:], in_=view[:, ts * width:te * width])
 
         ident = consts.tile([P, P], F32, name="ident")
         make_identity(nc, ident[:])
+        ident_bf = consts.tile([P, P], BF16, name="ident_bf")
+        make_identity(nc, ident_bf[:])
+
+        warm = consts.tile([P, 4], F32, name="warm")
+        nc.scalar.activation(out=warm[:, 0:1], in_=bz[:, 0:1], func=IDENTITY, bias=0.0, scale=1.0)
 
         bzf = consts.tile([P, P], F32, name="bzf")
         nc.vector.tensor_copy(out=bzf[:], in_=bz[:])
-        pb = ps_a.tile([P, 2, 256], F32, name="pb", tag="a")
-        nc.tensor.transpose(pb[:, 0, 0:P], bzf[:], ident[:])
-        bias = consts.tile([P, 4], F32, name="bias")
-        nc.vector.tensor_copy(out=bias[:, 0:3], in_=pb[:, 0, 0:3])
-
         w32 = w_sb[:].bitcast(F32)
         wg = consts.tile([P, 3 * G], BF16, name="wg", align_bytes=64)
         wg32 = wg[:].bitcast(F32).rearrange("p (f u) -> p f u", u=2)
@@ -101,14 +131,19 @@ def tile_painnmixing_pb_t_kernel(tc, h, mu_W, mu_VW, q, mu, W2, b2, out_0, out_1
                 scales=ws[:, f0 * P:(f0 + nj) * P],
                 in_=wg[:, f0 * G:(f0 + nj) * G],
             )
+        pb = ps_b.tile([P, TMAX * P], F32, name="pb", tag="b")
+        nc.tensor.transpose(pb[:, 0:P], bzf[:], ident[:])
+        bias = consts.tile([P, 4], F32, name="bias")
+        nc.vector.tensor_copy(out=bias[:, 0:3], in_=pb[:, 0:3])
 
-        g_t, hc_t, hs_t, xb_t, c_t, mo_t, qo_t = {}, {}, {}, {}, {}, {}, {}
+        g_t, hc_t, hs_t, xb_t, c_t = {}, {}, {}, {}, {}
 
         def fwd(c):
-            h32 = h_sb[c][:].bitcast(F32)
-            g = work.tile([P, T * G], BF16, name="g", tag="g", align_bytes=64)
+            nt = CHUNKS[c][1]
+            h32 = chunk_view(h_p, c, G).bitcast(F32)
+            g = work.tile([P, TMAX * G], BF16, name="g", tag="g", align_bytes=64)
             g32 = g[:].bitcast(F32).rearrange("p (a u) -> p a u", u=2)
-            for hb in range(T // 2):
+            for hb in range(nt // 2):
                 pa = ps_a.tile([P, 2, 256], F32, name="pa", tag="a")
                 for tl in range(2):
                     for u in range(2):
@@ -121,77 +156,128 @@ def tile_painnmixing_pb_t_kernel(tc, h, mu_W, mu_VW, q, mu, W2, b2, out_0, out_1
             g_t[c] = g
 
         def quant(c):
-            hc = work.tile([P, T * P], U32, name="hc", tag="hc", align_bytes=64)
-            hs = work.tile([P, T * P], U8, name="hs", tag="hs", align_bytes=64)
-            nc.vector.quantize_mx(out=hc[:].bitcast(FP8X4), scales=hs[:], in_=g_t[c][:])
+            nt = CHUNKS[c][1]
+            hc = work.tile([P, TMAX * P], U32, name="hc", tag="hc", align_bytes=64)
+            hs = work.tile([P, TMAX * P], U8, name="hs", tag="hs", align_bytes=64)
+            nc.vector.quantize_mx(
+                out=hc[:, 0:nt * P].bitcast(FP8X4), scales=hs[:, 0:nt * P], in_=g_t[c][:, 0:nt * G]
+            )
             hc_t[c] = hc
             hs_t[c] = hs
 
         def mx(c):
-            xb = work.tile([P, 3, T * P], F32, name="xb", tag="xb")
-            for j in BLOCK_ORDER:
-                pbk = ps_b.tile([P, T * P], F32, name="pbk", tag="b")
+            nt = CHUNKS[c][1]
+            xb = work.tile([P, 3, TMAX * P], F32, name="xb", tag="xb")
+            for j in (1, 2, 0):
+                pbk = ps_b.tile([P, TMAX * P], F32, name="pbk", tag="b")
                 nc.tensor.matmul_mx(
-                    out=pbk[:],
+                    out=pbk[:, 0:nt * P],
                     lhsT=wc[:, j * P:(j + 1) * P].bitcast(FP8X4),
                     lhsT_scale=ws[:, j * P:(j + 1) * P],
-                    rhs=hc_t[c][:].bitcast(FP8X4),
-                    rhs_scale=hs_t[c][:],
+                    rhs=hc_t[c][:, 0:nt * P].bitcast(FP8X4),
+                    rhs_scale=hs_t[c][:, 0:nt * P],
                     start=True,
                     stop=True,
                 )
-                nc.scalar.activation(out=xb[:, j, :], in_=pbk[:], func=IDENTITY, bias=bias[:, j:j + 1], scale=1.0)
+                nc.scalar.activation(
+                    out=xb[:, j, 0:nt * P], in_=pbk[:, 0:nt * P], func=IDENTITY, bias=bias[:, j:j + 1], scale=1.0
+                )
             xb_t[c] = xb
 
-        def back(c):
-            for j in BLOCK_ORDER:
-                pc = ps_c.tile([P, T, P], F32, name="pc", tag="c")
-                for t in range(T):
+        def back(c, j):
+            nt = CHUNKS[c][1]
+            pc = ps_c.tile([P, TMAX, P], F32, name="pc%d" % j, tag="c%d" % j)
+            if j == 0:
+                nc.tensor.matmul(
+                    out=pc[:, 0:nt, :].rearrange("p t f -> p (t f)"),
+                    lhsT=ident_bf[:],
+                    rhs=chunk_view(q_p, c, F),
+                    start=True,
+                    stop=False,
+                )
+                for t in range(nt):
+                    nc.tensor.matmul(
+                        out=pc[:, t, :],
+                        lhsT=xb_t[c][:, j, t * P:(t + 1) * P],
+                        rhs=ident[:],
+                        is_transpose=True,
+                        start=False,
+                        stop=(t == nt - 1),
+                    )
+            else:
+                for t in range(nt):
                     nc.tensor.transpose(pc[:, t, :], xb_t[c][:, j, t * P:(t + 1) * P], ident[:])
-                c_t[(c, j)] = pc
+            c_t[(c, j)] = pc
 
-        def ew1(c):
-            mo = res.tile([P, T * C * F], F32, name="mo%d" % c)
-            qo = res.tile([P, T * F], F32, name="qo%d" % c)
-            v = work.tile([P, T * F], F32, name="v", tag="v")
+        def op_mul_vec(c):
+            nt = CHUNKS[c][1]
             nc.vector.tensor_tensor(
-                out=mo[:].rearrange("p (t c f) -> p t c f", t=T, c=C),
-                in0=c_t[(c, 1)][:].unsqueeze(2).to_broadcast([P, T, C, F]),
-                in1=muw_sb[c][:].rearrange("p (t c f) -> p t c f", t=T, c=C),
+                out=chunk_view(mo_p, c, C * F).rearrange("p (t c f) -> p t c f", t=nt, c=C),
+                in0=c_t[(c, 1)][:, 0:nt, :].unsqueeze(2).to_broadcast([P, nt, C, F]),
+                in1=chunk_view(muw_p, c, C * F).rearrange("p (t c f) -> p t c f", t=nt, c=C),
                 op=MULT,
             )
-            nc.vector.tensor_tensor(
-                out=qo[:], in0=c_t[(c, 2)][:].rearrange("p t f -> p (t f)"), in1=muvw_sb[c][:], op=MULT
-            )
-            nc.vector.tensor_tensor(
-                out=v[:], in0=c_t[(c, 0)][:].rearrange("p t f -> p (t f)"), in1=q_sb[c][:], op=ADD
-            )
-            mo_t[c] = mo
-            qo_t[c] = (qo, v)
 
-        def ew2(c):
-            t0 = c * T
-            mo = mo_t[c]
-            qo, v = qo_t[c]
-            nc.vector.tensor_tensor(out=mo[:], in0=mo[:], in1=mu_sb[c][:], op=ADD)
-            nc.sync.dma_start(out=o1_v[:, t0 * C * F:(t0 + T) * C * F], in_=mo[:])
-            nc.vector.tensor_tensor(out=qo[:], in0=qo[:], in1=v[:], op=ADD)
-            nc.sync.dma_start(out=o0_v[:, t0 * F:(t0 + T) * F], in_=qo[:])
+        def op_mul_sca(c):
+            nt = CHUNKS[c][1]
+            nc.vector.tensor_tensor(
+                out=chunk_view(qo_p, c, F),
+                in0=c_t[(c, 2)][:, 0:nt, :].rearrange("p t f -> p (t f)"),
+                in1=chunk_view(muvw_p, c, F),
+                op=MULT,
+            )
+
+        def op_add_sca(c):
+            nt = CHUNKS[c][1]
+            nc.vector.tensor_tensor(
+                out=chunk_view(qo_p, c, F),
+                in0=c_t[(c, 0)][:, 0:nt, :].rearrange("p t f -> p (t f)"),
+                in1=chunk_view(qo_p, c, F),
+                op=ADD,
+            )
+
+        def op_add_vec(c, engine):
+            engine.tensor_tensor(
+                out=chunk_view(mo_p, c, C * F),
+                in0=chunk_view(mo_p, c, C * F),
+                in1=chunk_view(mu_p, c, C * F),
+                op=ADD,
+            )
+
+        def store(tiles, c, view, width):
+            t1 = CHUNKS[c][0] + CHUNKS[c][1]
+            for ts, te, tl in tiles:
+                if te == t1:
+                    nc.sync.dma_start(out=view[:, ts * width:te * width], in_=tl[:])
 
         fwd(0)
         quant(0)
-        fwd(1)
         mx(0)
+        fwd(1)
+        for j in (1, 2, 0):
+            back(0, j)
         quant(1)
-        back(0)
         for c in range(NCH):
+            last = c == NCH - 1
             if c + 2 < NCH:
                 fwd(c + 2)
-            if c + 1 < NCH:
+            if not last:
                 mx(c + 1)
-            ew1(c)
+            op_mul_vec(c)
+            if last:
+                op_add_vec(c, nc.vector)
+                store(mo_p, c, o1_v, C * F)
+            else:
+                back(c + 1, 1)
+            op_mul_sca(c)
+            if not last:
+                back(c + 1, 2)
+            op_add_sca(c)
+            if not last:
+                back(c + 1, 0)
             if c + 2 < NCH:
                 quant(c + 2)
-            if c + 1 < NCH:
-                back(c + 1)
-            ew2(c)
+            store(qo_p, c, o0_v, F)
+            if not last:
+                op_add_vec(c, nc.gpsimd)
+                store(mo_p, c, o1_v, C * F)

@@ -275,9 +275,9 @@ def tile_painnmixing_pb_t_kernel(tc, h, mu_W, mu_VW, q, mu, W2, b2, out_0, out_1
             op_add_sca(c)
             if not last:
                 back(c + 1, 0)
-            if c + 2 < NCH:
-                quant(c + 2)
             store(qo_p, c, o0_v, F)
             if not last:
-                op_add_vec(c, nc.gpsimd)
+                op_add_vec(c, nc.vector)
                 store(mo_p, c, o1_v, C * F)
+            if c + 2 < NCH:
+                quant(c + 2)

@@ -20,21 +20,20 @@ G = 512
 F = 128
 C = 3
 TPP = ATOMS // P
-CHUNKS = ((0, 2), (2, 2), (4, 4), (8, 4), (12, 4), (16, 4), (20, 4), (24, 4), (28, 2), (30, 2))
-NCH = len(CHUNKS)
-TMAX = 4
+T = 4
+NCH = TPP // T
 
-H_PIECES = ((0, 2), (2, 4), (4, 8), (8, 12), (12, 20), (20, 28), (28, 32))
-VEC_PIECES = ((0, 2), (2, 4), (4, 8), (8, 12), (12, 20), (20, 28), (28, 32))
+H_PIECES = ((0, 4), (4, 8), (8, 12), (12, 16), (16, 24), (24, 28), (28, 32))
+VEC_PIECES = ((0, 4), (4, 8), (8, 12), (12, 16), (16, 24), (24, 28), (28, 32))
 SCA_PIECES = ((0, 4), (4, 12), (12, 32))
-MO_PIECES = ((0, 8), (8, 16), (16, 24), (24, 28), (28, 30), (30, 32))
+MO_PIECES = ((0, 8), (8, 16), (16, 24), (24, 28), (28, 32))
 QO_PIECES = ((0, 16), (16, 28), (28, 32))
 LOAD_ORDER = (
-    ("h", 0), ("muw", 0), ("h", 1), ("q", 0), ("muvw", 0), ("mu", 0),
-    ("h", 2), ("muw", 1), ("mu", 1),
-    ("h", 3), ("muw", 2), ("q", 1), ("muvw", 1), ("mu", 2),
-    ("h", 4), ("muw", 3), ("mu", 3),
-    ("muw", 4), ("q", 2), ("muvw", 2), ("mu", 4),
+    ("h", 0), ("muvw", 0), ("q", 0), ("h", 1), ("muw", 0), ("mu", 0),
+    ("h", 2), ("muvw", 1), ("q", 1), ("muw", 1), ("mu", 1),
+    ("h", 3), ("muw", 2), ("mu", 2),
+    ("h", 4), ("muvw", 2), ("q", 2), ("muw", 3), ("mu", 3),
+    ("muw", 4), ("mu", 4),
     ("h", 5), ("muw", 5), ("mu", 5),
     ("h", 6), ("muw", 6), ("mu", 6),
 )
@@ -66,10 +65,10 @@ def tile_painnmixing_pb_t_kernel(tc, h, mu_W, mu_VW, q, mu, W2, b2, out_0, out_1
             ]
 
         def chunk_view(tiles, c, width):
-            t0, nt = CHUNKS[c]
+            t0 = c * T
             for ts, te, tl in tiles:
-                if ts <= t0 and t0 + nt <= te:
-                    return tl[:, (t0 - ts) * width:(t0 - ts + nt) * width]
+                if ts <= t0 and t0 + T <= te:
+                    return tl[:, (t0 - ts) * width:(t0 - ts + T) * width]
             raise ValueError("chunk not inside a piece")
 
         h_p = make_pieces(H_PIECES, G, BF16, "h")
@@ -131,113 +130,103 @@ def tile_painnmixing_pb_t_kernel(tc, h, mu_W, mu_VW, q, mu, W2, b2, out_0, out_1
                 scales=ws[:, f0 * P:(f0 + nj) * P],
                 in_=wg[:, f0 * G:(f0 + nj) * G],
             )
-        pb = ps_b.tile([P, TMAX * P], F32, name="pb", tag="b")
+        pb = ps_b.tile([P, T * P], F32, name="pb", tag="b")
         nc.tensor.transpose(pb[:, 0:P], bzf[:], ident[:])
         bias = consts.tile([P, 4], F32, name="bias")
         nc.vector.tensor_copy(out=bias[:, 0:3], in_=pb[:, 0:3])
 
-        g_t, hc_t, hs_t, xb_t, c_t = {}, {}, {}, {}, {}
+        g_t, hc_t, hs_t, xb_t, ut_t, c1_t, c0_t, d_t = {}, {}, {}, {}, {}, {}, {}, {}
 
-        def fwd(c):
-            nt = CHUNKS[c][1]
+        def fwd(c, hb):
             h32 = chunk_view(h_p, c, G).bitcast(F32)
-            g = work.tile([P, TMAX * G], BF16, name="g", tag="g", align_bytes=64)
-            g32 = g[:].bitcast(F32).rearrange("p (a u) -> p a u", u=2)
-            for hb in range(nt // 2):
-                pa = ps_a.tile([P, 2, 256], F32, name="pa", tag="a")
-                for tl in range(2):
-                    for u in range(2):
-                        col = (hb * 2 + tl) * 256 + u * P
-                        nc.tensor.transpose(pa[:, u, tl * P:(tl + 1) * P], h32[:, col:col + P], ident[:])
-                nc.scalar.copy(
-                    out=g32[:, hb * 256:(hb + 1) * 256, :],
-                    in_=pa[:].rearrange("p u a -> p a u"),
-                )
-            g_t[c] = g
+            if hb == 0:
+                g_t[c] = work.tile([P, T * G], BF16, name="g", tag="g", align_bytes=64)
+            g32 = g_t[c][:].bitcast(F32).rearrange("p (a u) -> p a u", u=2)
+            pa = ps_a.tile([P, 2, 256], F32, name="pa", tag="a")
+            for tl in range(2):
+                for u in range(2):
+                    col = (hb * 2 + tl) * 256 + u * P
+                    nc.tensor.transpose(pa[:, u, tl * P:(tl + 1) * P], h32[:, col:col + P], ident[:])
+            nc.scalar.copy(
+                out=g32[:, hb * 256:(hb + 1) * 256, :],
+                in_=pa[:].rearrange("p u a -> p a u"),
+            )
 
         def quant(c):
-            nt = CHUNKS[c][1]
-            hc = work.tile([P, TMAX * P], U32, name="hc", tag="hc", align_bytes=64)
-            hs = work.tile([P, TMAX * P], U8, name="hs", tag="hs", align_bytes=64)
-            nc.vector.quantize_mx(
-                out=hc[:, 0:nt * P].bitcast(FP8X4), scales=hs[:, 0:nt * P], in_=g_t[c][:, 0:nt * G]
-            )
+            hc = work.tile([P, T * P], U32, name="hc", tag="hc", align_bytes=64)
+            hs = work.tile([P, T * P], U8, name="hs", tag="hs", align_bytes=64)
+            nc.vector.quantize_mx(out=hc[:].bitcast(FP8X4), scales=hs[:], in_=g_t[c][:])
             hc_t[c] = hc
             hs_t[c] = hs
 
-        def mx(c):
-            nt = CHUNKS[c][1]
-            xb = work.tile([P, 3, TMAX * P], F32, name="xb", tag="xb")
-            for j in (1, 2, 0):
-                pbk = ps_b.tile([P, TMAX * P], F32, name="pbk", tag="b")
-                nc.tensor.matmul_mx(
-                    out=pbk[:, 0:nt * P],
-                    lhsT=wc[:, j * P:(j + 1) * P].bitcast(FP8X4),
-                    lhsT_scale=ws[:, j * P:(j + 1) * P],
-                    rhs=hc_t[c][:, 0:nt * P].bitcast(FP8X4),
-                    rhs_scale=hs_t[c][:, 0:nt * P],
-                    start=True,
-                    stop=True,
-                )
-                nc.scalar.activation(
-                    out=xb[:, j, 0:nt * P], in_=pbk[:, 0:nt * P], func=IDENTITY, bias=bias[:, j:j + 1], scale=1.0
-                )
-            xb_t[c] = xb
+        def mx(c, j):
+            if j == 1:
+                xb_t[c] = work.tile([P, 3, T * P], F32, name="xb", tag="xb")
+            pbk = ps_b.tile([P, T * P], F32, name="pbk", tag="b")
+            nc.tensor.matmul_mx(
+                out=pbk[:],
+                lhsT=wc[:, j * P:(j + 1) * P].bitcast(FP8X4),
+                lhsT_scale=ws[:, j * P:(j + 1) * P],
+                rhs=hc_t[c][:].bitcast(FP8X4),
+                rhs_scale=hs_t[c][:],
+                start=True,
+                stop=True,
+            )
+            nc.scalar.activation(out=xb_t[c][:, j, :], in_=pbk[:], func=IDENTITY, bias=bias[:, j:j + 1], scale=1.0)
 
-        def back(c, j):
-            nt = CHUNKS[c][1]
-            pc = ps_c.tile([P, TMAX, P], F32, name="pc%d" % j, tag="c%d" % j)
-            if j == 0:
+        def muvw_transposes(c):
+            d = ps_c.tile([P, T * P], BF16, name="pd", tag="d")
+            src = chunk_view(muvw_p, c, F)
+            for t in range(T):
+                nc.tensor.transpose(d[:, t * P:(t + 1) * P], src[:, t * P:(t + 1) * P], ident_bf[:])
+            d_t[c] = d
+
+        def x1_back(c):
+            pc = ps_c.tile([P, T, P], F32, name="pc1", tag="c1")
+            for t in range(T):
+                nc.tensor.transpose(pc[:, t, :], xb_t[c][:, 1, t * P:(t + 1) * P], ident[:])
+            c1_t[c] = pc
+
+        def q_open(c):
+            pc = ps_c.tile([P, T, P], F32, name="pc0", tag="c0")
+            nc.tensor.matmul(
+                out=pc[:].rearrange("p t f -> p (t f)"),
+                lhsT=ident_bf[:],
+                rhs=chunk_view(q_p, c, F),
+                start=True,
+                stop=False,
+            )
+            c0_t[c] = pc
+
+        def q_add(c, src, closes):
+            for t in range(T):
                 nc.tensor.matmul(
-                    out=pc[:, 0:nt, :].rearrange("p t f -> p (t f)"),
-                    lhsT=ident_bf[:],
-                    rhs=chunk_view(q_p, c, F),
-                    start=True,
-                    stop=False,
+                    out=c0_t[c][:, t, :],
+                    lhsT=src[:, t * P:(t + 1) * P],
+                    rhs=ident[:],
+                    is_transpose=True,
+                    start=False,
+                    stop=(closes and t == T - 1),
                 )
-                for t in range(nt):
-                    nc.tensor.matmul(
-                        out=pc[:, t, :],
-                        lhsT=xb_t[c][:, j, t * P:(t + 1) * P],
-                        rhs=ident[:],
-                        is_transpose=True,
-                        start=False,
-                        stop=(t == nt - 1),
-                    )
-            else:
-                for t in range(nt):
-                    nc.tensor.transpose(pc[:, t, :], xb_t[c][:, j, t * P:(t + 1) * P], ident[:])
-            c_t[(c, j)] = pc
+
+        def q_out(c):
+            nc.scalar.copy(out=chunk_view(qo_p, c, F), in_=c0_t[c][:].rearrange("p t f -> p (t f)"))
+
+        def op_u(c):
+            ut = work.tile([P, T * P], F32, name="ut", tag="ut")
+            nc.vector.tensor_tensor(out=ut[:], in0=xb_t[c][:, 2, :], in1=d_t[c][:], op=MULT)
+            ut_t[c] = ut
 
         def op_mul_vec(c):
-            nt = CHUNKS[c][1]
             nc.vector.tensor_tensor(
-                out=chunk_view(mo_p, c, C * F).rearrange("p (t c f) -> p t c f", t=nt, c=C),
-                in0=c_t[(c, 1)][:, 0:nt, :].unsqueeze(2).to_broadcast([P, nt, C, F]),
-                in1=chunk_view(muw_p, c, C * F).rearrange("p (t c f) -> p t c f", t=nt, c=C),
+                out=chunk_view(mo_p, c, C * F).rearrange("p (t c f) -> p t c f", t=T, c=C),
+                in0=c1_t[c][:].unsqueeze(2).to_broadcast([P, T, C, F]),
+                in1=chunk_view(muw_p, c, C * F).rearrange("p (t c f) -> p t c f", t=T, c=C),
                 op=MULT,
             )
 
-        def op_mul_sca(c):
-            nt = CHUNKS[c][1]
+        def op_add_vec(c):
             nc.vector.tensor_tensor(
-                out=chunk_view(qo_p, c, F),
-                in0=c_t[(c, 2)][:, 0:nt, :].rearrange("p t f -> p (t f)"),
-                in1=chunk_view(muvw_p, c, F),
-                op=MULT,
-            )
-
-        def op_add_sca(c):
-            nt = CHUNKS[c][1]
-            nc.vector.tensor_tensor(
-                out=chunk_view(qo_p, c, F),
-                in0=c_t[(c, 0)][:, 0:nt, :].rearrange("p t f -> p (t f)"),
-                in1=chunk_view(qo_p, c, F),
-                op=ADD,
-            )
-
-        def op_add_vec(c, engine):
-            engine.tensor_tensor(
                 out=chunk_view(mo_p, c, C * F),
                 in0=chunk_view(mo_p, c, C * F),
                 in1=chunk_view(mu_p, c, C * F),
@@ -245,39 +234,45 @@ def tile_painnmixing_pb_t_kernel(tc, h, mu_W, mu_VW, q, mu, W2, b2, out_0, out_1
             )
 
         def store(tiles, c, view, width):
-            t1 = CHUNKS[c][0] + CHUNKS[c][1]
+            t1 = (c + 1) * T
             for ts, te, tl in tiles:
                 if te == t1:
                     nc.sync.dma_start(out=view[:, ts * width:te * width], in_=tl[:])
 
-        fwd(0)
+        fwd(0, 0)
+        fwd(0, 1)
+        fwd(1, 0)
+        fwd(1, 1)
         quant(0)
-        mx(0)
-        fwd(1)
-        for j in (1, 2, 0):
-            back(0, j)
-        quant(1)
+        mx(0, 1)
+        mx(0, 2)
+        muvw_transposes(0)
+        x1_back(0)
+        mx(0, 0)
+        q_open(0)
+        op_u(0)
         for c in range(NCH):
             last = c == NCH - 1
-            if c + 2 < NCH:
-                fwd(c + 2)
             if not last:
-                mx(c + 1)
-            op_mul_vec(c)
-            if last:
-                op_add_vec(c, nc.vector)
-                store(mo_p, c, o1_v, C * F)
-            else:
-                back(c + 1, 1)
-            op_mul_sca(c)
-            if not last:
-                back(c + 1, 2)
-            op_add_sca(c)
-            if not last:
-                back(c + 1, 0)
+                quant(c + 1)
+            q_add(c, xb_t[c][:, 0, :], False)
+            q_add(c, ut_t[c][:], True)
+            q_out(c)
             store(qo_p, c, o0_v, F)
-            if not last:
-                op_add_vec(c, nc.vector)
-                store(mo_p, c, o1_v, C * F)
             if c + 2 < NCH:
-                quant(c + 2)
+                fwd(c + 2, 0)
+            if not last:
+                mx(c + 1, 1)
+                mx(c + 1, 2)
+            op_mul_vec(c)
+            if c + 2 < NCH:
+                fwd(c + 2, 1)
+            if not last:
+                muvw_transposes(c + 1)
+                x1_back(c + 1)
+                mx(c + 1, 0)
+                q_open(c + 1)
+            op_add_vec(c)
+            store(mo_p, c, o1_v, C * F)
+            if not last:
+                op_u(c + 1)

@@ -23,20 +23,8 @@ TPP = ATOMS // P
 T = 4
 NCH = TPP // T
 
-H_PIECES = ((0, 4), (4, 8), (8, 12), (12, 16), (16, 24), (24, 28), (28, 32))
-VEC_PIECES = ((0, 4), (4, 8), (8, 12), (12, 16), (16, 24), (24, 28), (28, 32))
-SCA_PIECES = ((0, 4), (4, 12), (12, 32))
-MO_PIECES = ((0, 8), (8, 16), (16, 24), (24, 28), (28, 32))
-QO_PIECES = ((0, 16), (16, 28), (28, 32))
-LOAD_ORDER = (
-    ("h", 0), ("muvw", 0), ("q", 0), ("h", 1), ("muw", 0), ("mu", 0),
-    ("h", 2), ("muvw", 1), ("q", 1), ("muw", 1), ("mu", 1),
-    ("h", 3), ("muw", 2), ("mu", 2),
-    ("h", 4), ("muvw", 2), ("q", 2), ("muw", 3), ("mu", 3),
-    ("muw", 4), ("mu", 4),
-    ("h", 5), ("muw", 5), ("mu", 5),
-    ("h", 6), ("muw", 6), ("mu", 6),
-)
+IN_PIECES = ((0, 4), (4, 8), (8, 16), (16, 24), (24, 32))
+OUT_PIECES = ((0, 8), (8, 16), (16, 24), (24, 28), (28, 32))
 
 
 def tile_painnmixing_pb_t_kernel(tc, h, mu_W, mu_VW, q, mu, W2, b2, out_0, out_1):
@@ -71,13 +59,17 @@ def tile_painnmixing_pb_t_kernel(tc, h, mu_W, mu_VW, q, mu, W2, b2, out_0, out_1
                     return tl[:, (t0 - ts) * width:(t0 - ts + T) * width]
             raise ValueError("chunk not inside a piece")
 
-        h_p = make_pieces(H_PIECES, G, BF16, "h")
-        muw_p = make_pieces(VEC_PIECES, C * F, BF16, "muw")
-        mu_p = make_pieces(VEC_PIECES, C * F, BF16, "mu")
-        muvw_p = make_pieces(SCA_PIECES, F, BF16, "muvw")
-        q_p = make_pieces(SCA_PIECES, F, BF16, "q")
-        mo_p = make_pieces(MO_PIECES, C * F, F32, "mo")
-        qo_p = make_pieces(QO_PIECES, F, F32, "qo")
+        h_p = make_pieces(IN_PIECES, G, BF16, "h")
+        muw_p = make_pieces(IN_PIECES, C * F, BF16, "muw")
+        mu_p = make_pieces(IN_PIECES, C * F, BF16, "mu")
+        muvw_p = make_pieces(IN_PIECES, F, BF16, "muvw")
+        q_p = make_pieces(IN_PIECES, F, BF16, "q")
+        mo_p = make_pieces(OUT_PIECES, C * F, F32, "mo")
+        qo_p = make_pieces(OUT_PIECES, F, F32, "qo")
+
+        def load(tiles, i, view, width):
+            ts, te, tl = tiles[i]
+            nc.sync.dma_start(out=tl[:], in_=view[:, ts * width:te * width])
 
         bz = consts.tile([P, P], BF16, name="bz")
         nc.vector.memset(bz[:], 0.0)
@@ -87,17 +79,14 @@ def tile_painnmixing_pb_t_kernel(tc, h, mu_W, mu_VW, q, mu, W2, b2, out_0, out_1
             out=w_sb[:].rearrange("p (j k) -> p j k", j=3),
             in_=W2.rearrange("(j p) k -> p j k", p=P),
         )
-        sources = {
-            "h": (h_p, h_v, G),
-            "muw": (muw_p, muw_v, C * F),
-            "mu": (mu_p, mu_v, C * F),
-            "muvw": (muvw_p, muvw_v, F),
-            "q": (q_p, q_v, F),
-        }
-        for key, i in LOAD_ORDER:
-            tiles, view, width = sources[key]
-            ts, te, tl = tiles[i]
-            nc.sync.dma_start(out=tl[:], in_=view[:, ts * width:te * width])
+        load(h_p, 0, h_v, G)
+        for i in range(len(IN_PIECES)):
+            if i + 1 < len(IN_PIECES):
+                load(h_p, i + 1, h_v, G)
+            load(muvw_p, i, muvw_v, F)
+            load(q_p, i, q_v, F)
+            load(muw_p, i, muw_v, C * F)
+            load(mu_p, i, mu_v, C * F)
 
         ident = consts.tile([P, P], F32, name="ident")
         make_identity(nc, ident[:])
@@ -115,7 +104,7 @@ def tile_painnmixing_pb_t_kernel(tc, h, mu_W, mu_VW, q, mu, W2, b2, out_0, out_1
         wc = consts.tile([P, 3 * F], U32, name="wc", align_bytes=64)
         ws = consts.tile([P, 3 * F], U8, name="ws", align_bytes=64)
         for f0, nj in ((0, 2), (2, 1)):
-            pw = ps_a.tile([P, 2, 256], F32, name="pw", tag="a")
+            pw = ps_b.tile([P, 2, 256], F32, name="pw", tag="b")
             for jl in range(nj):
                 for u in range(2):
                     col = (f0 + jl) * 256 + u * P
@@ -160,7 +149,7 @@ def tile_painnmixing_pb_t_kernel(tc, h, mu_W, mu_VW, q, mu, W2, b2, out_0, out_1
             hs_t[c] = hs
 
         def mx(c, j):
-            if j == 1:
+            if c not in xb_t:
                 xb_t[c] = work.tile([P, 3, T * P], F32, name="xb", tag="xb")
             pbk = ps_b.tile([P, T * P], F32, name="pbk", tag="b")
             nc.tensor.matmul_mx(
@@ -244,8 +233,8 @@ def tile_painnmixing_pb_t_kernel(tc, h, mu_W, mu_VW, q, mu, W2, b2, out_0, out_1
         fwd(1, 0)
         fwd(1, 1)
         quant(0)
-        mx(0, 1)
         mx(0, 2)
+        mx(0, 1)
         muvw_transposes(0)
         x1_back(0)
         mx(0, 0)
@@ -255,15 +244,15 @@ def tile_painnmixing_pb_t_kernel(tc, h, mu_W, mu_VW, q, mu, W2, b2, out_0, out_1
             last = c == NCH - 1
             if not last:
                 quant(c + 1)
+            if c + 2 < NCH:
+                fwd(c + 2, 0)
+            if not last:
+                mx(c + 1, 2)
+                mx(c + 1, 1)
             q_add(c, xb_t[c][:, 0, :], False)
             q_add(c, ut_t[c][:], True)
             q_out(c)
             store(qo_p, c, o0_v, F)
-            if c + 2 < NCH:
-                fwd(c + 2, 0)
-            if not last:
-                mx(c + 1, 1)
-                mx(c + 1, 2)
             op_mul_vec(c)
             if c + 2 < NCH:
                 fwd(c + 2, 1)

@@ -25,6 +25,7 @@ NCH = TPP // T
 
 IN_PIECES = ((0, 4), (4, 8), (8, 16), (16, 24), (24, 32))
 OUT_PIECES = ((0, 8), (8, 16), (16, 24), (24, 28), (28, 32))
+MU_OUT_PIECES = ((0, 8), (8, 16), (16, 24), (24, 28), (28, 30), (30, 32))
 
 
 def tile_painnmixing_pb_t_kernel(tc, h, mu_W, mu_VW, q, mu, W2, b2, out_0, out_1):
@@ -52,19 +53,21 @@ def tile_painnmixing_pb_t_kernel(tc, h, mu_W, mu_VW, q, mu, W2, b2, out_0, out_1
                 for ts, te in pieces
             ]
 
-        def chunk_view(tiles, c, width):
-            t0 = c * T
+        def span(tiles, t_lo, t_hi, width):
             for ts, te, tl in tiles:
-                if ts <= t0 and t0 + T <= te:
-                    return tl[:, (t0 - ts) * width:(t0 - ts + T) * width]
-            raise ValueError("chunk not inside a piece")
+                if ts <= t_lo and t_hi <= te:
+                    return tl[:, (t_lo - ts) * width:(t_hi - ts) * width]
+            raise ValueError("range not inside a piece")
+
+        def chunk_view(tiles, c, width):
+            return span(tiles, c * T, (c + 1) * T, width)
 
         h_p = make_pieces(IN_PIECES, G, BF16, "h")
         muw_p = make_pieces(IN_PIECES, C * F, BF16, "muw")
         mu_p = make_pieces(IN_PIECES, C * F, BF16, "mu")
         muvw_p = make_pieces(IN_PIECES, F, BF16, "muvw")
         q_p = make_pieces(IN_PIECES, F, BF16, "q")
-        mo_p = make_pieces(OUT_PIECES, C * F, F32, "mo")
+        mo_p = make_pieces(MU_OUT_PIECES, C * F, F32, "mo")
         qo_p = make_pieces(OUT_PIECES, F, F32, "qo")
 
         def load(tiles, i, view, width):
@@ -206,24 +209,24 @@ def tile_painnmixing_pb_t_kernel(tc, h, mu_W, mu_VW, q, mu, W2, b2, out_0, out_1
             nc.vector.tensor_tensor(out=ut[:], in0=xb_t[c][:, 2, :], in1=d_t[c][:], op=MULT)
             ut_t[c] = ut
 
-        def op_mul_vec(c):
+        def op_mul_vec(c, lo, hi):
+            n = hi - lo
             nc.vector.tensor_tensor(
-                out=chunk_view(mo_p, c, C * F).rearrange("p (t c f) -> p t c f", t=T, c=C),
-                in0=c1_t[c][:].unsqueeze(2).to_broadcast([P, T, C, F]),
-                in1=chunk_view(muw_p, c, C * F).rearrange("p (t c f) -> p t c f", t=T, c=C),
+                out=span(mo_p, c * T + lo, c * T + hi, C * F).rearrange("p (t c f) -> p t c f", t=n, c=C),
+                in0=c1_t[c][:, lo:hi, :].unsqueeze(2).to_broadcast([P, n, C, F]),
+                in1=span(muw_p, c * T + lo, c * T + hi, C * F).rearrange("p (t c f) -> p t c f", t=n, c=C),
                 op=MULT,
             )
 
-        def op_add_vec(c):
-            nc.vector.tensor_tensor(
-                out=chunk_view(mo_p, c, C * F),
-                in0=chunk_view(mo_p, c, C * F),
-                in1=chunk_view(mu_p, c, C * F),
+        def op_add_vec(c, lo, hi, engine):
+            engine.tensor_tensor(
+                out=span(mo_p, c * T + lo, c * T + hi, C * F),
+                in0=span(mo_p, c * T + lo, c * T + hi, C * F),
+                in1=span(mu_p, c * T + lo, c * T + hi, C * F),
                 op=ADD,
             )
 
-        def store(tiles, c, view, width):
-            t1 = (c + 1) * T
+        def store(tiles, t1, view, width):
             for ts, te, tl in tiles:
                 if te == t1:
                     nc.sync.dma_start(out=view[:, ts * width:te * width], in_=tl[:])
@@ -249,19 +252,25 @@ def tile_painnmixing_pb_t_kernel(tc, h, mu_W, mu_VW, q, mu, W2, b2, out_0, out_1
             if not last:
                 mx(c + 1, 2)
                 mx(c + 1, 1)
+                muvw_transposes(c + 1)
             q_add(c, xb_t[c][:, 0, :], False)
             q_add(c, ut_t[c][:], True)
             q_out(c)
-            store(qo_p, c, o0_v, F)
-            op_mul_vec(c)
-            if c + 2 < NCH:
-                fwd(c + 2, 1)
-            if not last:
-                muvw_transposes(c + 1)
+            store(qo_p, (c + 1) * T, o0_v, F)
+            if last:
+                for lo in (0, 2):
+                    op_mul_vec(c, lo, lo + 2)
+                    op_add_vec(c, lo, lo + 2, nc.vector)
+                    store(mo_p, c * T + lo + 2, o1_v, C * F)
+            else:
+                op_mul_vec(c, 0, 1)
+                op_add_vec(c, 0, 1, nc.gpsimd)
+                op_mul_vec(c, 1, T)
+                if c + 2 < NCH:
+                    fwd(c + 2, 1)
                 x1_back(c + 1)
                 mx(c + 1, 0)
                 q_open(c + 1)
-            op_add_vec(c)
-            store(mo_p, c, o1_v, C * F)
-            if not last:
                 op_u(c + 1)
+                op_add_vec(c, 1, T, nc.vector)
+                store(mo_p, (c + 1) * T, o1_v, C * F)

@@ -24,7 +24,8 @@ T = 4
 NCH = TPP // T
 
 IN_PIECES = ((0, 4), (4, 8), (8, 16), (16, 24), (24, 32))
-OUT_PIECES = ((0, 8), (8, 16), (16, 24), (24, 28), (28, 32))
+SCALAR_IN_PIECES = ((0, 8), (8, 32))
+Q_OUT_PIECES = ((0, 16), (16, 28), (28, 32))
 MU_OUT_PIECES = ((0, 8), (8, 16), (16, 24), (24, 28), (28, 30), (30, 32))
 
 
@@ -65,10 +66,10 @@ def tile_painnmixing_pb_t_kernel(tc, h, mu_W, mu_VW, q, mu, W2, b2, out_0, out_1
         h_p = make_pieces(IN_PIECES, G, BF16, "h")
         muw_p = make_pieces(IN_PIECES, C * F, BF16, "muw")
         mu_p = make_pieces(IN_PIECES, C * F, BF16, "mu")
-        muvw_p = make_pieces(IN_PIECES, F, BF16, "muvw")
-        q_p = make_pieces(IN_PIECES, F, BF16, "q")
+        muvw_p = make_pieces(SCALAR_IN_PIECES, F, BF16, "muvw")
+        q_p = make_pieces(SCALAR_IN_PIECES, F, BF16, "q")
         mo_p = make_pieces(MU_OUT_PIECES, C * F, F32, "mo")
-        qo_p = make_pieces(OUT_PIECES, F, F32, "qo")
+        qo_p = make_pieces(Q_OUT_PIECES, F, F32, "qo")
 
         def load(tiles, i, view, width):
             ts, te, tl = tiles[i]
@@ -86,8 +87,10 @@ def tile_painnmixing_pb_t_kernel(tc, h, mu_W, mu_VW, q, mu, W2, b2, out_0, out_1
         for i in range(len(IN_PIECES)):
             if i + 1 < len(IN_PIECES):
                 load(h_p, i + 1, h_v, G)
-            load(muvw_p, i, muvw_v, F)
-            load(q_p, i, q_v, F)
+            for j in range(len(SCALAR_IN_PIECES)):
+                if SCALAR_IN_PIECES[j][0] == IN_PIECES[i][0]:
+                    load(muvw_p, j, muvw_v, F)
+                    load(q_p, j, q_v, F)
             load(muw_p, i, muw_v, C * F)
             load(mu_p, i, mu_v, C * F)
 

from contextlib import ExitStack

import concourse.mybir as mybir
from concourse.masks import make_identity

FLOPS = 2 * 4096 * 512 * 384

F32 = mybir.dt.float32
BF16 = mybir.dt.bfloat16
U32 = mybir.dt.uint32
U8 = mybir.dt.uint8
FP8X4 = mybir.dt.float8_e4m3fn_x4
MULT = mybir.AluOpType.mult
ADD = mybir.AluOpType.add
IDENTITY = mybir.ActivationFunctionType.Identity

P = 128
ATOMS = 4096
G = 512
F = 128
C = 3
TPP = ATOMS // P
T = 4
NCH = TPP // T

IN_PIECES = ((0, 4), (4, 8), (8, 16), (16, 24), (24, 32))
SCALAR_IN_PIECES = ((0, 8), (8, 32))
Q_OUT_PIECES = ((0, 16), (16, 28), (28, 32))
MU_OUT_PIECES = ((0, 8), (8, 16), (16, 24), (24, 28), (28, 30), (30, 32))


def tile_painnmixing_pb_t_kernel(tc, h, mu_W, mu_VW, q, mu, W2, b2, out_0, out_1):
    nc = tc.nc
    h_v = h.rearrange("(p t) o k -> p (t o k)", t=TPP)
    muw_v = mu_W.rearrange("(p t) c f -> p (t c f)", t=TPP)
    muvw_v = mu_VW.rearrange("(p t) o f -> p (t o f)", t=TPP)
    q_v = q.rearrange("(p t) o f -> p (t o f)", t=TPP)
    mu_v = mu.rearrange("(p t) c f -> p (t c f)", t=TPP)
    o0_v = out_0.rearrange("(p t) o f -> p (t o f)", t=TPP)
    o1_v = out_1.rearrange("(p t) c f -> p (t c f)", t=TPP)

    with ExitStack() as ctx:
        ctx.enter_context(tc.manual_schedule())
        consts = ctx.enter_context(tc.tile_pool(name="consts", bufs=1))
        res = ctx.enter_context(tc.tile_pool(name="res", bufs=1))
        work = ctx.enter_context(tc.tile_pool(name="work", bufs=2))
        ps_a = ctx.enter_context(tc.psum_pool(name="ps_a", bufs=2))
        ps_b = ctx.enter_context(tc.psum_pool(name="ps_b", bufs=3))
        ps_c = ctx.enter_context(tc.psum_pool(name="ps_c", bufs=1))

        def make_pieces(pieces, width, dtype, label):
            return [
                (ts, te, res.tile([P, (te - ts) * width], dtype, name="%s%d" % (label, ts)))
                for ts, te in pieces
            ]

        def span(tiles, t_lo, t_hi, width):
            for ts, te, tl in tiles:
                if ts <= t_lo and t_hi <= te:
                    return tl[:, (t_lo - ts) * width:(t_hi - ts) * width]
            raise ValueError("range not inside a piece")

        def chunk_view(tiles, c, width):
            return span(tiles, c * T, (c + 1) * T, width)

        h_p = make_pieces(IN_PIECES, G, BF16, "h")
        muw_p = make_pieces(IN_PIECES, C * F, BF16, "muw")
        mu_p = make_pieces(IN_PIECES, C * F, BF16, "mu")
        muvw_p = make_pieces(SCALAR_IN_PIECES, F, BF16, "muvw")
        q_p = make_pieces(SCALAR_IN_PIECES, F, BF16, "q")
        mo_p = make_pieces(MU_OUT_PIECES, C * F, F32, "mo")
        qo_p = make_pieces(Q_OUT_PIECES, F, F32, "qo")

        def load(tiles, i, view, width):
            ts, te, tl = tiles[i]
            nc.sync.dma_start(out=tl[:], in_=view[:, ts * width:te * width])

        bz = consts.tile([P, P], BF16, name="bz")
        nc.vector.memset(bz[:], 0.0)
        nc.scalar.dma_start(out=bz[0:3, :], in_=b2.rearrange("(j f) -> j f", j=3))
        w_sb = consts.tile([P, 3 * G], BF16, name="w_sb")
        nc.sync.dma_start(
            out=w_sb[:].rearrange("p (j k) -> p j k", j=3),
            in_=W2.rearrange("(j p) k -> p j k", p=P),
        )
        load(h_p, 0, h_v, G)
        for i in range(len(IN_PIECES)):
            if i + 1 < len(IN_PIECES):
                load(h_p, i + 1, h_v, G)
            for j in range(len(SCALAR_IN_PIECES)):
                if SCALAR_IN_PIECES[j][0] == IN_PIECES[i][0]:
                    load(muvw_p, j, muvw_v, F)
                    load(q_p, j, q_v, F)
            load(muw_p, i, muw_v, C * F)
            load(mu_p, i, mu_v, C * F)

        ident = consts.tile([P, P], F32, name="ident")
        make_identity(nc, ident[:])
        ident_bf = consts.tile([P, P], BF16, name="ident_bf")
        make_identity(nc, ident_bf[:])

        warm = consts.tile([P, 4], F32, name="warm")
        nc.scalar.activation(out=warm[:, 0:1], in_=bz[:, 0:1], func=IDENTITY, bias=0.0, scale=1.0)

        bzf = consts.tile([P, P], F32, name="bzf")
        nc.vector.tensor_copy(out=bzf[:], in_=bz[:])
        w32 = w_sb[:].bitcast(F32)
        wg = consts.tile([P, 3 * G], BF16, name="wg", align_bytes=64)
        wg32 = wg[:].bitcast(F32).rearrange("p (f u) -> p f u", u=2)
        wc = consts.tile([P, 3 * F], U32, name="wc", align_bytes=64)
        ws = consts.tile([P, 3 * F], U8, name="ws", align_bytes=64)
        for f0, nj in ((0, 2), (2, 1)):
            pw = ps_b.tile([P, 2, 256], F32, name="pw", tag="b")
            for jl in range(nj):
                for u in range(2):
                    col = (f0 + jl) * 256 + u * P
                    nc.tensor.transpose(pw[:, u, jl * P:(jl + 1) * P], w32[:, col:col + P], ident[:])
            nc.vector.tensor_copy(
                out=wg32[:, f0 * P:(f0 + nj) * P, :],
                in_=pw[:, :, 0:nj * P].rearrange("p u a -> p a u"),
            )
        for f0, nj in ((0, 2), (2, 1)):
            nc.vector.quantize_mx(
                out=wc[:, f0 * P:(f0 + nj) * P].bitcast(FP8X4),
                scales=ws[:, f0 * P:(f0 + nj) * P],
                in_=wg[:, f0 * G:(f0 + nj) * G],
            )
        pb = ps_b.tile([P, T * P], F32, name="pb", tag="b")
        nc.tensor.transpose(pb[:, 0:P], bzf[:], ident[:])
        bias = consts.tile([P, 4], F32, name="bias")
        nc.vector.tensor_copy(out=bias[:, 0:3], in_=pb[:, 0:3])

        g_t, hc_t, hs_t, xb_t, ut_t, c1_t, c0_t, d_t = {}, {}, {}, {}, {}, {}, {}, {}

        def fwd(c, hb):
            h32 = chunk_view(h_p, c, G).bitcast(F32)
            if hb == 0:
                g_t[c] = work.tile([P, T * G], BF16, name="g", tag="g", align_bytes=64)
            g32 = g_t[c][:].bitcast(F32).rearrange("p (a u) -> p a u", u=2)
            pa = ps_a.tile([P, 2, 256], F32, name="pa", tag="a")
            for tl in range(2):
                for u in range(2):
                    col = (hb * 2 + tl) * 256 + u * P
                    nc.tensor.transpose(pa[:, u, tl * P:(tl + 1) * P], h32[:, col:col + P], ident[:])
            nc.scalar.copy(
                out=g32[:, hb * 256:(hb + 1) * 256, :],
                in_=pa[:].rearrange("p u a -> p a u"),
            )

        def quant(c):
            hc = work.tile([P, T * P], U32, name="hc", tag="hc", align_bytes=64)
            hs = work.tile([P, T * P], U8, name="hs", tag="hs", align_bytes=64)
            nc.vector.quantize_mx(out=hc[:].bitcast(FP8X4), scales=hs[:], in_=g_t[c][:])
            hc_t[c] = hc
            hs_t[c] = hs

        def mx(c, j):
            if c not in xb_t:
                xb_t[c] = work.tile([P, 3, T * P], F32, name="xb", tag="xb")
            pbk = ps_b.tile([P, T * P], F32, name="pbk", tag="b")
            nc.tensor.matmul_mx(
                out=pbk[:],
                lhsT=wc[:, j * P:(j + 1) * P].bitcast(FP8X4),
                lhsT_scale=ws[:, j * P:(j + 1) * P],
                rhs=hc_t[c][:].bitcast(FP8X4),
                rhs_scale=hs_t[c][:],
                start=True,
                stop=True,
            )
            nc.scalar.activation(out=xb_t[c][:, j, :], in_=pbk[:], func=IDENTITY, bias=bias[:, j:j + 1], scale=1.0)

        def muvw_transposes(c):
            d = ps_c.tile([P, T * P], BF16, name="pd", tag="d")
            src = chunk_view(muvw_p, c, F)
            for t in range(T):
                nc.tensor.transpose(d[:, t * P:(t + 1) * P], src[:, t * P:(t + 1) * P], ident_bf[:])
            d_t[c] = d

        def x1_back(c):
            pc = ps_c.tile([P, T, P], F32, name="pc1", tag="c1")
            for t in range(T):
                nc.tensor.transpose(pc[:, t, :], xb_t[c][:, 1, t * P:(t + 1) * P], ident[:])
            c1_t[c] = pc

        def q_open(c):
            pc = ps_c.tile([P, T, P], F32, name="pc0", tag="c0")
            nc.tensor.matmul(
                out=pc[:].rearrange("p t f -> p (t f)"),
                lhsT=ident_bf[:],
                rhs=chunk_view(q_p, c, F),
                start=True,
                stop=False,
            )
            c0_t[c] = pc

        def q_add(c, src, closes):
            for t in range(T):
                nc.tensor.matmul(
                    out=c0_t[c][:, t, :],
                    lhsT=src[:, t * P:(t + 1) * P],
                    rhs=ident[:],
                    is_transpose=True,
                    start=False,
                    stop=(closes and t == T - 1),
                )

        def q_out(c):
            nc.scalar.copy(out=chunk_view(qo_p, c, F), in_=c0_t[c][:].rearrange("p t f -> p (t f)"))

        def op_u(c):
            ut = work.tile([P, T * P], F32, name="ut", tag="ut")
            nc.vector.tensor_tensor(out=ut[:], in0=xb_t[c][:, 2, :], in1=d_t[c][:], op=MULT)
            ut_t[c] = ut

        def op_mul_vec(c, lo, hi):
            n = hi - lo
            nc.vector.tensor_tensor(
                out=span(mo_p, c * T + lo, c * T + hi, C * F).rearrange("p (t c f) -> p t c f", t=n, c=C),
                in0=c1_t[c][:, lo:hi, :].unsqueeze(2).to_broadcast([P, n, C, F]),
                in1=span(muw_p, c * T + lo, c * T + hi, C * F).rearrange("p (t c f) -> p t c f", t=n, c=C),
                op=MULT,
            )

        def op_add_vec(c, lo, hi, engine):
            engine.tensor_tensor(
                out=span(mo_p, c * T + lo, c * T + hi, C * F),
                in0=span(mo_p, c * T + lo, c * T + hi, C * F),
                in1=span(mu_p, c * T + lo, c * T + hi, C * F),
                op=ADD,
            )

        def store(tiles, t1, view, width):
            for ts, te, tl in tiles:
                if te == t1:
                    nc.sync.dma_start(out=view[:, ts * width:te * width], in_=tl[:])

        fwd(0, 0)
        fwd(0, 1)
        fwd(1, 0)
        fwd(1, 1)
        quant(0)
        mx(0, 2)
        mx(0, 1)
        muvw_transposes(0)
        x1_back(0)
        mx(0, 0)
        q_open(0)
        op_u(0)
        for c in range(NCH):
            last = c == NCH - 1
            if not last:
                quant(c + 1)
            if c + 2 < NCH:
                fwd(c + 2, 0)
            if not last:
                mx(c + 1, 2)
                mx(c + 1, 1)
                muvw_transposes(c + 1)
            q_add(c, xb_t[c][:, 0, :], False)
            q_add(c, ut_t[c][:], True)
            q_out(c)
            store(qo_p, (c + 1) * T, o0_v, F)
            if last:
                for lo in (0, 2):
                    op_mul_vec(c, lo, lo + 2)
                    op_add_vec(c, lo, lo + 2, nc.vector)
                    store(mo_p, c * T + lo + 2, o1_v, C * F)
            else:
                op_mul_vec(c, 0, 1)
                op_add_vec(c, 0, 1, nc.gpsimd)
                op_mul_vec(c, 1, T)
                if c + 2 < NCH:
                    fwd(c + 2, 1)
                x1_back(c + 1)
                mx(c + 1, 0)
                q_open(c + 1)
                op_u(c + 1)
                op_add_vec(c, 1, T, nc.vector)
                store(mo_p, (c + 1) * T, o1_v, C * F)
